import numpy as np
import ml_dtypes


def mxq(x, axis, fmt="e4m3"):
    dtype, down = {"e4m3": (ml_dtypes.float8_e4m3fn, 7), "e5m2": (ml_dtypes.float8_e5m2, 14)}[fmt]
    v = np.moveaxis(np.asarray(x, np.float32).astype(ml_dtypes.bfloat16).astype(np.float64), axis, -1)
    blocks = v.reshape(v.shape[:-1] + (-1, 32))
    amax = np.abs(blocks).max(-1, keepdims=True)
    byte = np.maximum(np.where(amax > 0, np.frexp(amax)[1] - 1 + 127, 0) - down, 1)
    scale = np.exp2(byte - 127.0)
    codes = (blocks / scale).astype(np.float32).astype(dtype).astype(np.float64)
    return np.moveaxis((codes * scale).reshape(v.shape), -1, axis)


WIDE = False


def mx_kscale(k):
    if not WIDE:
        return np.ones(k)
    levels = np.array([10, -10, 5, -5, 0])
    a = np.random.permutation(np.resize(levels, k // 512 * 4)).reshape(k // 512, 4)
    idx = np.arange(k)
    return np.exp2(a[idx // 512, idx % 128 // 32])


BF16 = ml_dtypes.bfloat16


def bf(x):
    return np.asarray(x, np.float32).astype(BF16)


def f64(x):
    return np.asarray(x).astype(np.float64)


E2M1 = np.array([0.0, 0.5, 1.0, 1.5, 2.0, 3.0, 4.0, 6.0, -0.0, -0.5, -1.0, -1.5, -2.0, -3.0, -4.0, -6.0])


def pack_weight(w, fmt):
    k, n = w.shape
    w = f64(bf(w)).reshape(k // 32, 32, n)
    amax = np.abs(w).max(1)
    if fmt == "e4m3":
        byte = np.frexp(amax)[1] - 1 + 127 - 7
    else:
        mant, ex = np.frexp(amax / 6.0)
        byte = np.where(mant > 0.5, ex, ex - 1) + 127
    byte = np.clip(np.where(amax > 0, byte, 1), 1, 254)
    scaled = (w * np.exp2(127.0 - byte)[:, None, :]).reshape(k, n).astype(np.float32)
    by_word = np.ascontiguousarray(scaled.reshape(k // 512, 128, 4, n).transpose(0, 1, 3, 2))
    if fmt == "e4m3":
        words = by_word.astype(ml_dtypes.float8_e4m3fn).view(np.uint8)
    else:
        c = by_word.astype(ml_dtypes.float4_e2m1fn).view(np.uint8) & 0xF
        words = c[..., 0::2] | (c[..., 1::2] << 4)
    return np.ascontiguousarray(words), np.ascontiguousarray(byte.astype(np.uint8).reshape(k // 512, 16, n))


def unpack_weight(words, scales, fmt):
    g, p, n, _ = words.shape
    if fmt == "e4m3":
        vals = np.ascontiguousarray(words).view(ml_dtypes.float8_e4m3fn).astype(np.float64)
    else:
        nib = np.empty((g, p, n, 4), np.uint8)
        nib[..., 0::2] = words & 0xF
        nib[..., 1::2] = words >> 4
        vals = E2M1[nib]
    vals = vals * np.repeat(np.exp2(scales.astype(np.float64) - 127.0), 8, axis=1)[..., None]
    return vals.transpose(0, 1, 3, 2).reshape(g * 512, n)

def pack4(w):
    words, scales = pack_weight(w, "e2m1")
    return words.reshape(words.shape[0], 128, -1), scales


def unpack4(words, scales):
    return unpack_weight(words.reshape(words.shape[0], 128, -1, 2), scales, "e2m1")


B, IN, H = 512, 1024, 1024


def hard_sigmoid(v):
    return np.clip(v / 6.0 + 0.5, 0.0, 1.0)


def hard_tanh(v):
    return np.clip(v, -1.0, 1.0)


def setup_inputs():
    s, t = mx_kscale(IN), mx_kscale(H)
    input_ = bf(np.random.standard_normal((B, IN)) * s)
    h_0 = bf(np.random.standard_normal((B, H)) * t)
    c_0 = bf(np.random.standard_normal((B, H)))
    W_ih = np.random.standard_normal((4 * H, IN)) * 1.25 / np.sqrt(IN) / s[None, :]
    W_hh = np.random.standard_normal((4 * H, H)) * 1.25 / np.sqrt(H) / t[None, :]
    b_hh = bf(np.random.standard_normal(4 * H) * 0.3)
    W_ih_words, W_ih_scales = pack4(np.ascontiguousarray(W_ih.T))
    W_hh_words, W_hh_scales = pack4(np.ascontiguousarray(W_hh.T))
    return {"input_": input_,
            "h_0": h_0,
            "c_0": c_0,
            "W_ih_words": W_ih_words,
            "W_ih_scales": W_ih_scales,
            "W_hh_words": W_hh_words,
            "W_hh_scales": W_hh_scales,
            "b_hh": b_hh}


def reference(input_, h_0, c_0, W_ih_words, W_ih_scales, W_hh_words, W_hh_scales, b_hh):
    wi = mxq(f64(input_), 1, "e4m3") @ unpack4(W_ih_words, W_ih_scales)
    wh_b = (mxq(f64(h_0), 1, "e4m3") @ unpack4(W_hh_words, W_hh_scales)) + f64(b_hh)
    h_x4 = wh_b + wi
    f, i, o, g = np.split(h_x4, 4, axis=1)
    new = hard_sigmoid(i) * hard_tanh(g)
    old = hard_sigmoid(f) * f64(c_0)
    c_1 = old + new
    h_1 = hard_sigmoid(o) * hard_tanh(c_1)
    return (h_1, c_1)

@@ -1,0 +1,204 @@
+from contextlib import ExitStack
+
+import concourse.mybir as mybir
+from concourse.masks import make_identity
+
+F32 = mybir.dt.float32
+BF16 = mybir.dt.bfloat16
+I32 = mybir.dt.int32
+U32 = mybir.dt.uint32
+U8 = mybir.dt.uint8
+FP8X4 = mybir.dt.float8_e4m3fn_x4
+FP4X4 = mybir.dt.float4_e2m1fn_x4
+ALU = mybir.AluOpType
+ACT = mybir.ActivationFunctionType
+
+P = 128
+BATCH = 512
+K = 1024
+H = 1024
+M_TILES = BATCH // P
+K_PASS = 4 * P
+GROUPS = K // K_PASS
+PASSES = 2 * GROUPS
+N_TILE = 512
+HALVES = H // N_TILE
+F_GATE, I_GATE, O_GATE, G_GATE = 0, 1, 2, 3
+GATE_ORDER = (I_GATE, G_GATE, F_GATE, O_GATE)
+LAG = 1
+
+FLOPS = 2 * BATCH * (2 * K) * (4 * H)
+
+
+def tile_qlstmcell_kernel(
+    tc, input_, h_0, c_0, W_ih_words, W_ih_scales, W_hh_words, W_hh_scales, b_hh, out_0, out_1
+):
+    nc = tc.nc
+    acts = (input_, h_0)
+    w_words = (W_ih_words, W_hh_words)
+    w_scales = (W_ih_scales, W_hh_scales)
+
+    with ExitStack() as ctx:
+        keep = ctx.enter_context(tc.tile_pool(name="keep", bufs=1))
+        stage = ctx.enter_context(tc.tile_pool(name="stage", bufs=M_TILES))
+        brief = ctx.enter_context(tc.tile_pool(name="brief", bufs=4))
+        waiting = ctx.enter_context(tc.tile_pool(name="waiting", bufs=M_TILES + 2))
+        results = ctx.enter_context(tc.tile_pool(name="results", bufs=M_TILES * HALVES))
+        psum = ctx.enter_context(tc.psum_pool(name="psum", bufs=8))
+
+        act_sb = keep.tile([P, 2, M_TILES, K], BF16)
+        act_codes = keep.tile([P, M_TILES, PASSES * P], U32, align_bytes=64)
+        act_planes = keep.tile([P, M_TILES, PASSES * P], U8, align_bytes=64)
+        w_sb = keep.tile([P, PASSES, 2 * 4 * H], U8, align_bytes=64)
+        w_planes = keep.tile([P, PASSES, 4 * H], U8, align_bytes=64)
+        bias_sb = keep.tile([P, 4 * H], BF16)
+        c0_sb = keep.tile([P, M_TILES, H], BF16)
+        ident = keep.tile([P, P], F32)
+
+        nc.vector.memset(w_planes[:].bitcast(I32), 0)
+        make_identity(nc, ident[:])
+
+        for m in range(M_TILES):
+            for a in range(2):
+                nc.sync.dma_start(out=act_sb[:, a, m, :], in_=acts[a][m * P : (m + 1) * P, :])
+
+        def first_col(gate, j):
+            return gate * H + j * N_TILE
+
+        def load_scales(j):
+            for a in range(2):
+                for g in range(GROUPS):
+                    plane = w_planes[:, GROUPS * a + g, :].rearrange("p (t j n) -> p t j n", t=4, j=HALVES)
+                    rows = w_scales[a][g].rearrange("(q r) (t j n) -> r q t j n", r=4, t=4, j=HALVES)
+                    for r in range(4):
+                        nc.sync.dma_start(
+                            out=plane[r:P:32, :, j, :].bitcast(I32), in_=rows[r, :, :, j, :].bitcast(I32)
+                        )
+
+        def load_weights(j, gate):
+            lo = first_col(gate, j)
+            some_bytes = slice(2 * lo, 2 * (lo + N_TILE))
+            for a in range(2):
+                nc.sync.dma_start(
+                    out=w_sb[:, GROUPS * a : GROUPS * (a + 1), some_bytes].bitcast(I32),
+                    in_=w_words[a][:, :, some_bytes].bitcast(I32).rearrange("g p n -> p g n"),
+                )
+
+        def load_bias(j):
+            for gate in GATE_ORDER:
+                lo = first_col(gate, j)
+                cols = slice(lo, lo + N_TILE)
+                nc.sync.dma_start(out=bias_sb[:, cols], in_=b_hh[cols].partition_broadcast(P))
+
+        def load_c0(j):
+            cols = slice(j * N_TILE, (j + 1) * N_TILE)
+            nc.sync.dma_start(out=c0_sb[:, :, cols], in_=c_0.rearrange("(m p) h -> p m h", p=P)[:, :, cols])
+
+        for j in range(HALVES):
+            load_scales(j)
+            load_weights(j, GATE_ORDER[0])
+            load_bias(j)
+            load_weights(j, GATE_ORDER[1])
+            load_c0(j)
+            load_weights(j, GATE_ORDER[2])
+            load_weights(j, GATE_ORDER[3])
+
+        grouped = {}
+
+        def flip(m):
+            grouped[m] = stage.tile([P, 2, K], BF16, name="grouped", align_bytes=64)
+            for a in range(2):
+                words = act_sb[:, a, m, :].bitcast(F32)
+                flipped = psum.tile([P, GROUPS, 2, P], F32, name="flipped", tag="bank")
+                for g in range(GROUPS):
+                    for u in range(2):
+                        nc.tensor.transpose(
+                            flipped[:, g, u, :], words[:, 2 * P * g + u : 2 * P * (g + 1) : 2], ident[:]
+                        )
+                dst = grouped[m][:, a, :].bitcast(F32).rearrange("p (g r u) -> p g r u", g=GROUPS, u=2)
+                src = flipped[:].rearrange("p g u r -> p g r u")
+                if a == 0:
+                    nc.vector.tensor_copy(out=dst, in_=src)
+                else:
+                    nc.scalar.copy(out=dst, in_=src)
+
+        def quantise(m):
+            nc.vector.quantize_mx(
+                out=act_codes[:, m, :].bitcast(FP8X4),
+                scales=act_planes[:, m, :],
+                in_=grouped[m][:].rearrange("p a k -> p (a k)"),
+            )
+
+        for m in range(M_TILES + 1):
+            if m < M_TILES:
+                flip(m)
+            if m > 0:
+                quantise(m - 1)
+
+        summed = {}
+        gate_i = {}
+        fresh = {}
+        cell_t = {}
+
+        def open_bank(j, gate, m):
+            acc = psum.tile([P, N_TILE], F32, name="acc", tag="bank")
+            lo = first_col(gate, j)
+            cols = slice(lo, lo + N_TILE)
+            for c in range(PASSES):
+                nc.tensor.matmul_mx(
+                    out=acc[:],
+                    lhsT=act_codes[:, m, c * P : (c + 1) * P].bitcast(FP8X4),
+                    lhsT_scale=act_planes[:, m, c * P : (c + 1) * P],
+                    rhs=w_sb[:, c, 2 * lo : 2 * (lo + N_TILE)].bitcast(FP4X4),
+                    rhs_scale=w_planes[:, c, cols],
+                    start=(c == 0),
+                    stop=(c == PASSES - 1),
+                )
+            z = brief.tile([P, N_TILE], F32, name="z")
+            nc.vector.tensor_tensor(out=z[:], in0=acc[:], in1=bias_sb[:, cols], op=ALU.add)
+            if gate == G_GATE:
+                summed[m] = z
+            elif gate == I_GATE:
+                gate_i[m] = waiting.tile([P, N_TILE], F32, name="gate_i")
+                nc.scalar.activation(out=gate_i[m][:], in_=z[:], func=ACT.Relu, bias=0.5, scale=1.0 / 6.0)
+            else:
+                summed[m] = brief.tile([P, N_TILE], F32, name="relu")
+                nc.scalar.activation(out=summed[m][:], in_=z[:], func=ACT.Relu, bias=0.5, scale=1.0 / 6.0)
+
+        def close_bank(j, gate, m):
+            rows = slice(m * P, (m + 1) * P)
+            cols = slice(j * N_TILE, (j + 1) * N_TILE)
+            if gate == G_GATE:
+                tanh_g = brief.tile([P, N_TILE], F32, name="tanh_g")
+                nc.vector.tensor_scalar(
+                    out=tanh_g[:], in0=summed[m][:], scalar1=1.0, scalar2=-1.0, op0=ALU.min, op1=ALU.max
+                )
+                fresh[m] = waiting.tile([P, N_TILE], F32, name="fresh")
+                nc.vector.scalar_tensor_tensor(
+                    out=fresh[m][:], in0=gate_i[m][:], scalar=1.0, in1=tanh_g[:], op0=ALU.min, op1=ALU.mult
+                )
+            elif gate == F_GATE:
+                kept = brief.tile([P, N_TILE], F32, name="kept")
+                nc.vector.scalar_tensor_tensor(
+                    out=kept[:], in0=summed[m][:], scalar=1.0, in1=c0_sb[:, m, cols], op0=ALU.min, op1=ALU.mult
+                )
+                c_1 = results.tile([P, N_TILE], F32, name="c_1")
+                nc.gpsimd.tensor_tensor(out=c_1[:], in0=kept[:], in1=fresh[m][:], op=ALU.add)
+                nc.sync.dma_start(out=out_1[rows, cols], in_=c_1[:])
+                cell_t[m] = waiting.tile([P, N_TILE], F32, name="cell_t")
+                nc.gpsimd.tensor_scalar(
+                    out=cell_t[m][:], in0=c_1[:], scalar1=1.0, scalar2=-1.0, op0=ALU.min, op1=ALU.max
+                )
+            elif gate == O_GATE:
+                h_1 = results.tile([P, N_TILE], F32, name="h_1")
+                nc.vector.scalar_tensor_tensor(
+                    out=h_1[:], in0=summed[m][:], scalar=1.0, in1=cell_t[m][:], op0=ALU.min, op1=ALU.mult
+                )
+                nc.sync.dma_start(out=out_0[rows, cols], in_=h_1[:])
+
+        banks = [(j, gate, m) for j in range(HALVES) for gate in GATE_ORDER for m in range(M_TILES)]
+        for n in range(len(banks) + LAG):
+            if n < len(banks):
+                open_bank(*banks[n])
+            if n >= LAG:
+                close_bank(*banks[n - LAG])

@@ -24,8 +24,7 @@ PASSES = 2 * GROUPS
 N_TILE = 512
 HALVES = H // N_TILE
 F_GATE, I_GATE, O_GATE, G_GATE = 0, 1, 2, 3
-GATE_ORDER = (I_GATE, G_GATE, F_GATE, O_GATE)
-LAG = 1
+GATE_ORDER = (G_GATE, I_GATE, F_GATE, O_GATE)
 
 FLOPS = 2 * BATCH * (2 * K) * (4 * H)
 
@@ -41,21 +40,29 @@ def tile_qlstmcell_kernel(
     with ExitStack() as ctx:
         keep = ctx.enter_context(tc.tile_pool(name="keep", bufs=1))
         stage = ctx.enter_context(tc.tile_pool(name="stage", bufs=M_TILES))
-        brief = ctx.enter_context(tc.tile_pool(name="brief", bufs=4))
-        waiting = ctx.enter_context(tc.tile_pool(name="waiting", bufs=M_TILES + 2))
+        sums = ctx.enter_context(tc.tile_pool(name="sums", bufs=6))
+        cellwise = ctx.enter_context(tc.tile_pool(name="cellwise", bufs=2))
         results = ctx.enter_context(tc.tile_pool(name="results", bufs=M_TILES * HALVES))
         psum = ctx.enter_context(tc.psum_pool(name="psum", bufs=8))
+        ctx.enter_context(tc.manual_schedule())
 
         act_sb = keep.tile([P, 2, M_TILES, K], BF16)
         act_codes = keep.tile([P, M_TILES, PASSES * P], U32, align_bytes=64)
         act_planes = keep.tile([P, M_TILES, PASSES * P], U8, align_bytes=64)
-        w_sb = keep.tile([P, PASSES, 2 * 4 * H], U8, align_bytes=64)
-        w_planes = keep.tile([P, PASSES, 4 * H], U8, align_bytes=64)
-        bias_sb = keep.tile([P, 4 * H], BF16)
-        c0_sb = keep.tile([P, M_TILES, H], BF16)
         ident = keep.tile([P, P], F32)
+        w_sb = {}
+        bias_sb = {}
+        w_planes = {}
+        c0_sb = {}
+        for j in range(HALVES):
+            w_planes[j] = keep.tile([P, PASSES, 4, N_TILE], U8, name="w_planes%d" % j, align_bytes=64)
+            c0_sb[j] = keep.tile([P, M_TILES, N_TILE], BF16, name="c0_sb%d" % j)
+            for gate in GATE_ORDER:
+                w_sb[(j, gate)] = keep.tile([P, PASSES, 2 * N_TILE], U8, name="w_sb%d_%d" % (j, gate), align_bytes=64)
+                bias_sb[(j, gate)] = keep.tile([P, N_TILE], BF16, name="bias_sb%d_%d" % (j, gate))
 
-        nc.vector.memset(w_planes[:].bitcast(I32), 0)
+        for j in range(HALVES):
+            nc.vector.memset(w_planes[j][:].bitcast(I32), 0)
         make_identity(nc, ident[:])
 
         for m in range(M_TILES):
@@ -68,40 +75,34 @@ def tile_qlstmcell_kernel(
         def load_scales(j):
             for a in range(2):
                 for g in range(GROUPS):
-                    plane = w_planes[:, GROUPS * a + g, :].rearrange("p (t j n) -> p t j n", t=4, j=HALVES)
+                    plane = w_planes[j][:, GROUPS * a + g, :, :]
                     rows = w_scales[a][g].rearrange("(q r) (t j n) -> r q t j n", r=4, t=4, j=HALVES)
                     for r in range(4):
-                        nc.sync.dma_start(
-                            out=plane[r:P:32, :, j, :].bitcast(I32), in_=rows[r, :, :, j, :].bitcast(I32)
-                        )
+                        nc.sync.dma_start(out=plane[r:P:32, :, :].bitcast(I32), in_=rows[r, :, :, j, :].bitcast(I32))
 
         def load_weights(j, gate):
             lo = first_col(gate, j)
             some_bytes = slice(2 * lo, 2 * (lo + N_TILE))
             for a in range(2):
                 nc.sync.dma_start(
-                    out=w_sb[:, GROUPS * a : GROUPS * (a + 1), some_bytes].bitcast(I32),
+                    out=w_sb[(j, gate)][:, GROUPS * a : GROUPS * (a + 1), :].bitcast(I32),
                     in_=w_words[a][:, :, some_bytes].bitcast(I32).rearrange("g p n -> p g n"),
                 )
 
-        def load_bias(j):
-            for gate in GATE_ORDER:
-                lo = first_col(gate, j)
-                cols = slice(lo, lo + N_TILE)
-                nc.sync.dma_start(out=bias_sb[:, cols], in_=b_hh[cols].partition_broadcast(P))
+        def load_bias(j, gate):
+            lo = first_col(gate, j)
+            nc.sync.dma_start(out=bias_sb[(j, gate)][:], in_=b_hh[lo : lo + N_TILE].partition_broadcast(P))
 
         def load_c0(j):
             cols = slice(j * N_TILE, (j + 1) * N_TILE)
-            nc.sync.dma_start(out=c0_sb[:, :, cols], in_=c_0.rearrange("(m p) h -> p m h", p=P)[:, :, cols])
+            nc.sync.dma_start(out=c0_sb[j][:], in_=c_0.rearrange("(m p) h -> p m h", p=P)[:, :, cols])
 
         for j in range(HALVES):
             load_scales(j)
-            load_weights(j, GATE_ORDER[0])
-            load_bias(j)
-            load_weights(j, GATE_ORDER[1])
+            for gate in GATE_ORDER:
+                load_weights(j, gate)
+                load_bias(j, gate)
             load_c0(j)
-            load_weights(j, GATE_ORDER[2])
-            load_weights(j, GATE_ORDER[3])
 
         grouped = {}
 
@@ -135,70 +136,76 @@ def tile_qlstmcell_kernel(
             if m > 0:
                 quantise(m - 1)
 
-        summed = {}
-        gate_i = {}
-        fresh = {}
-        cell_t = {}
+        cells = [(j, m) for j in range(HALVES) for m in range(M_TILES)]
+        part = {}
 
-        def open_bank(j, gate, m):
+        def bank(n, gate):
+            j, m = cells[n]
             acc = psum.tile([P, N_TILE], F32, name="acc", tag="bank")
-            lo = first_col(gate, j)
-            cols = slice(lo, lo + N_TILE)
             for c in range(PASSES):
                 nc.tensor.matmul_mx(
                     out=acc[:],
                     lhsT=act_codes[:, m, c * P : (c + 1) * P].bitcast(FP8X4),
                     lhsT_scale=act_planes[:, m, c * P : (c + 1) * P],
-                    rhs=w_sb[:, c, 2 * lo : 2 * (lo + N_TILE)].bitcast(FP4X4),
-                    rhs_scale=w_planes[:, c, cols],
+                    rhs=w_sb[(j, gate)][:, c, :].bitcast(FP4X4),
+                    rhs_scale=w_planes[j][:, c, gate, :],
                     start=(c == 0),
                     stop=(c == PASSES - 1),
                 )
-            z = brief.tile([P, N_TILE], F32, name="z")
-            nc.vector.tensor_tensor(out=z[:], in0=acc[:], in1=bias_sb[:, cols], op=ALU.add)
+            z = sums.tile([P, N_TILE], F32, name="z")
+            nc.vector.tensor_tensor(out=z[:], in0=acc[:], in1=bias_sb[(j, gate)][:], op=ALU.add)
+            half_done = cellwise.tile([P, N_TILE], F32, name="half_done%d" % gate)
             if gate == G_GATE:
-                summed[m] = z
-            elif gate == I_GATE:
-                gate_i[m] = waiting.tile([P, N_TILE], F32, name="gate_i")
-                nc.scalar.activation(out=gate_i[m][:], in_=z[:], func=ACT.Relu, bias=0.5, scale=1.0 / 6.0)
+                nc.scalar.activation(out=half_done[:], in_=z[:], func=ACT.Relu, bias=1.0, scale=1.0)
+                nc.scalar.activation(out=half_done[:], in_=half_done[:], func=ACT.Relu, bias=2.0, scale=-1.0)
+                nc.scalar.activation(out=half_done[:], in_=half_done[:], func=ACT.Identity, bias=1.0, scale=-1.0)
             else:
-                summed[m] = brief.tile([P, N_TILE], F32, name="relu")
-                nc.scalar.activation(out=summed[m][:], in_=z[:], func=ACT.Relu, bias=0.5, scale=1.0 / 6.0)
+                nc.scalar.activation(out=half_done[:], in_=z[:], func=ACT.Relu, bias=0.5, scale=1.0 / 6.0)
+            part[(n, gate)] = half_done
 
-        def close_bank(j, gate, m):
-            rows = slice(m * P, (m + 1) * P)
-            cols = slice(j * N_TILE, (j + 1) * N_TILE)
-            if gate == G_GATE:
-                tanh_g = brief.tile([P, N_TILE], F32, name="tanh_g")
-                nc.vector.tensor_scalar(
-                    out=tanh_g[:], in0=summed[m][:], scalar1=1.0, scalar2=-1.0, op0=ALU.min, op1=ALU.max
-                )
-                fresh[m] = waiting.tile([P, N_TILE], F32, name="fresh")
-                nc.vector.scalar_tensor_tensor(
-                    out=fresh[m][:], in0=gate_i[m][:], scalar=1.0, in1=tanh_g[:], op0=ALU.min, op1=ALU.mult
-                )
-            elif gate == F_GATE:
-                kept = brief.tile([P, N_TILE], F32, name="kept")
-                nc.vector.scalar_tensor_tensor(
-                    out=kept[:], in0=summed[m][:], scalar=1.0, in1=c0_sb[:, m, cols], op0=ALU.min, op1=ALU.mult
-                )
-                c_1 = results.tile([P, N_TILE], F32, name="c_1")
-                nc.gpsimd.tensor_tensor(out=c_1[:], in0=kept[:], in1=fresh[m][:], op=ALU.add)
-                nc.sync.dma_start(out=out_1[rows, cols], in_=c_1[:])
-                cell_t[m] = waiting.tile([P, N_TILE], F32, name="cell_t")
-                nc.gpsimd.tensor_scalar(
-                    out=cell_t[m][:], in0=c_1[:], scalar1=1.0, scalar2=-1.0, op0=ALU.min, op1=ALU.max
-                )
-            elif gate == O_GATE:
-                h_1 = results.tile([P, N_TILE], F32, name="h_1")
-                nc.vector.scalar_tensor_tensor(
-                    out=h_1[:], in0=summed[m][:], scalar=1.0, in1=cell_t[m][:], op0=ALU.min, op1=ALU.mult
-                )
-                nc.sync.dma_start(out=out_0[rows, cols], in_=h_1[:])
+        def clipped_times(pool, n, name, gate, other):
+            part[(n, name)] = pool.tile([P, N_TILE], F32, name=name)
+            nc.vector.scalar_tensor_tensor(
+                out=part[(n, name)][:], in0=part[(n, gate)][:], scalar=1.0, in1=other, op0=ALU.min, op1=ALU.mult
+            )
 
-        banks = [(j, gate, m) for j in range(HALVES) for gate in GATE_ORDER for m in range(M_TILES)]
-        for n in range(len(banks) + LAG):
-            if n < len(banks):
-                open_bank(*banks[n])
-            if n >= LAG:
-                close_bank(*banks[n - LAG])
+        def store(n, name, out):
+            j, m = cells[n]
+            nc.sync.dma_start(
+                out=out[m * P : (m + 1) * P, j * N_TILE : (j + 1) * N_TILE], in_=part[(n, name)][:]
+            )
+
+        def new_cell_state(n):
+            part[(n, "c_1")] = results.tile([P, N_TILE], F32, name="c_1")
+            nc.vector.tensor_tensor(
+                out=part[(n, "c_1")][:], in0=part[(n, "kept")][:], in1=part[(n, "fresh")][:], op=ALU.add
+            )
+            store(n, "c_1", out_1)
+
+        def clip_cell_state(n):
+            part[(n, "tanh_c")] = cellwise.tile([P, N_TILE], F32, name="tanh_c")
+            nc.vector.tensor_scalar(
+                out=part[(n, "tanh_c")][:], in0=part[(n, "c_1")][:], scalar1=1.0, scalar2=-1.0, op0=ALU.min, op1=ALU.max
+            )
+
+        for n in range(len(cells) + 1):
+            opening = n < len(cells)
+            closing = n > 0
+            if opening:
+                bank(n, G_GATE)
+            if closing:
+                new_cell_state(n - 1)
+            if opening:
+                bank(n, I_GATE)
+            if closing:
+                clip_cell_state(n - 1)
+            if opening:
+                bank(n, F_GATE)
+            if closing:
+                clipped_times(results, n - 1, "h_1", O_GATE, part[(n - 1, "tanh_c")][:])
+                store(n - 1, "h_1", out_0)
+            if opening:
+                j, m = cells[n]
+                clipped_times(cellwise, n, "fresh", I_GATE, part[(n, G_GATE)][:])
+                bank(n, O_GATE)
+                clipped_times(cellwise, n, "kept", F_GATE, c0_sb[j][:, m, :])

@@ -194,18 +194,20 @@ def tile_qlstmcell_kernel(
             if opening:
                 bank(n, G_GATE)
             if closing:
-                new_cell_state(n - 1)
+                j, m = cells[n - 1]
+                clipped_times(cellwise, n - 1, "kept", F_GATE, c0_sb[j][:, m, :])
             if opening:
                 bank(n, I_GATE)
             if closing:
-                clip_cell_state(n - 1)
+                new_cell_state(n - 1)
             if opening:
                 bank(n, F_GATE)
+            if closing:
+                clip_cell_state(n - 1)
+            if opening:
+                bank(n, O_GATE)
             if closing:
                 clipped_times(results, n - 1, "h_1", O_GATE, part[(n - 1, "tanh_c")][:])
                 store(n - 1, "h_1", out_0)
             if opening:
-                j, m = cells[n]
                 clipped_times(cellwise, n, "fresh", I_GATE, part[(n, G_GATE)][:])
-                bank(n, O_GATE)
-                clipped_times(cellwise, n, "kept", F_GATE, c0_sb[j][:, m, :])

@@ -175,39 +175,32 @@ def tile_qlstmcell_kernel(
                 out=out[m * P : (m + 1) * P, j * N_TILE : (j + 1) * N_TILE], in_=part[(n, name)][:]
             )
 
-        def new_cell_state(n):
+        def new_cell_state(n, engine):
             part[(n, "c_1")] = results.tile([P, N_TILE], F32, name="c_1")
-            nc.vector.tensor_tensor(
+            engine.tensor_tensor(
                 out=part[(n, "c_1")][:], in0=part[(n, "kept")][:], in1=part[(n, "fresh")][:], op=ALU.add
             )
             store(n, "c_1", out_1)
-
-        def clip_cell_state(n):
             part[(n, "tanh_c")] = cellwise.tile([P, N_TILE], F32, name="tanh_c")
-            nc.vector.tensor_scalar(
+            engine.tensor_scalar(
                 out=part[(n, "tanh_c")][:], in0=part[(n, "c_1")][:], scalar1=1.0, scalar2=-1.0, op0=ALU.min, op1=ALU.max
             )
 
-        for n in range(len(cells) + 1):
-            opening = n < len(cells)
-            closing = n > 0
-            if opening:
-                bank(n, G_GATE)
-            if closing:
-                j, m = cells[n - 1]
-                clipped_times(cellwise, n - 1, "kept", F_GATE, c0_sb[j][:, m, :])
-            if opening:
-                bank(n, I_GATE)
-            if closing:
-                new_cell_state(n - 1)
-            if opening:
-                bank(n, F_GATE)
-            if closing:
-                clip_cell_state(n - 1)
-            if opening:
-                bank(n, O_GATE)
-            if closing:
-                clipped_times(results, n - 1, "h_1", O_GATE, part[(n - 1, "tanh_c")][:])
-                store(n - 1, "h_1", out_0)
-            if opening:
-                clipped_times(cellwise, n, "fresh", I_GATE, part[(n, G_GATE)][:])
+        def new_output(n):
+            clipped_times(results, n, "h_1", O_GATE, part[(n, "tanh_c")][:])
+            store(n, "h_1", out_0)
+
+        bank(0, G_GATE)
+        for n in range(len(cells)):
+            j, m = cells[n]
+            bank(n, I_GATE)
+            bank(n, F_GATE)
+            bank(n, O_GATE)
+            if n + 1 < len(cells):
+                bank(n + 1, G_GATE)
+            clipped_times(cellwise, n, "fresh", I_GATE, part[(n, G_GATE)][:])
+            clipped_times(cellwise, n, "kept", F_GATE, c0_sb[j][:, m, :])
+            if n > 0:
+                new_output(n - 1)
+            new_cell_state(n, nc.gpsimd if n + 1 < len(cells) else nc.vector)
+        new_output(len(cells) - 1)

@@ -52,6 +52,8 @@ def tile_qlstmcell_kernel(
         ident = keep.tile([P, P], F32)
         w_sb = {}
         bias_sb = {}
+        bias_row = keep.tile([P, 4 * H], BF16)
+        ones = keep.tile([P, P], BF16)
         w_planes = {}
         c0_sb = {}
         for j in range(HALVES):
@@ -59,15 +61,18 @@ def tile_qlstmcell_kernel(
             c0_sb[j] = keep.tile([P, M_TILES, N_TILE], BF16, name="c0_sb%d" % j)
             for gate in GATE_ORDER:
                 w_sb[(j, gate)] = keep.tile([P, PASSES, 2 * N_TILE], U8, name="w_sb%d_%d" % (j, gate), align_bytes=64)
-                bias_sb[(j, gate)] = keep.tile([P, N_TILE], BF16, name="bias_sb%d_%d" % (j, gate))
+                bias_sb[(j, gate)] = keep.tile([P, N_TILE], F32, name="bias_sb%d_%d" % (j, gate))
 
-        for j in range(HALVES):
-            nc.vector.memset(w_planes[j][:].bitcast(I32), 0)
+        nc.vector.memset(w_planes[0][:].bitcast(I32), 0)
+        nc.vector.memset(bias_row[:].bitcast(I32), 0)
+        nc.vector.memset(w_planes[1][:].bitcast(I32), 0)
         make_identity(nc, ident[:])
+        nc.gpsimd.memset(ones[:], 1.0)
 
         for m in range(M_TILES):
             for a in range(2):
                 nc.sync.dma_start(out=act_sb[:, a, m, :], in_=acts[a][m * P : (m + 1) * P, :])
+        nc.scalar.dma_start(out=bias_row[0:1, :], in_=b_hh.unsqueeze(0))
 
         def first_col(gate, j):
             return gate * H + j * N_TILE
@@ -89,19 +94,15 @@ def tile_qlstmcell_kernel(
                     in_=w_words[a][:, :, some_bytes].bitcast(I32).rearrange("g p n -> p g n"),
                 )
 
-        def load_bias(j, gate):
-            lo = first_col(gate, j)
-            nc.sync.dma_start(out=bias_sb[(j, gate)][:], in_=b_hh[lo : lo + N_TILE].partition_broadcast(P))
-
         def load_c0(j):
             cols = slice(j * N_TILE, (j + 1) * N_TILE)
             nc.sync.dma_start(out=c0_sb[j][:], in_=c_0.rearrange("(m p) h -> p m h", p=P)[:, :, cols])
 
         for j in range(HALVES):
+            load_weights(j, GATE_ORDER[0])
             load_scales(j)
-            for gate in GATE_ORDER:
+            for gate in GATE_ORDER[1:]:
                 load_weights(j, gate)
-                load_bias(j, gate)
             load_c0(j)
 
         grouped = {}
@@ -135,6 +136,13 @@ def tile_qlstmcell_kernel(
                 flip(m)
             if m > 0:
                 quantise(m - 1)
+
+        for j in range(HALVES):
+            for gate in GATE_ORDER:
+                lo = first_col(gate, j)
+                spread = psum.tile([P, N_TILE], F32, name="spread", tag="bank")
+                nc.tensor.matmul(spread[:], lhsT=ones[:], rhs=bias_row[:, lo : lo + N_TILE], start=True, stop=True)
+                nc.scalar.copy(out=bias_sb[(j, gate)][:], in_=spread[:])
 
         cells = [(j, m) for j in range(HALVES) for m in range(M_TILES)]
         part = {}
@@ -195,12 +203,12 @@ def tile_qlstmcell_kernel(
             j, m = cells[n]
             bank(n, I_GATE)
             bank(n, F_GATE)
-            bank(n, O_GATE)
             if n + 1 < len(cells):
                 bank(n + 1, G_GATE)
             clipped_times(cellwise, n, "fresh", I_GATE, part[(n, G_GATE)][:])
             clipped_times(cellwise, n, "kept", F_GATE, c0_sb[j][:, m, :])
             if n > 0:
                 new_output(n - 1)
+            bank(n, O_GATE)
             new_cell_state(n, nc.gpsimd if n + 1 < len(cells) else nc.vector)
         new_output(len(cells) - 1)

@@ -26,6 +26,8 @@ HALVES = H // N_TILE
 F_GATE, I_GATE, O_GATE, G_GATE = 0, 1, 2, 3
 GATE_ORDER = (G_GATE, I_GATE, F_GATE, O_GATE)
 
+G_AHEAD = M_TILES
+
 FLOPS = 2 * BATCH * (2 * K) * (4 * H)
 
 
@@ -42,6 +44,7 @@ def tile_qlstmcell_kernel(
         stage = ctx.enter_context(tc.tile_pool(name="stage", bufs=M_TILES))
         sums = ctx.enter_context(tc.tile_pool(name="sums", bufs=6))
         cellwise = ctx.enter_context(tc.tile_pool(name="cellwise", bufs=2))
+        ahead = ctx.enter_context(tc.tile_pool(name="ahead", bufs=G_AHEAD))
         results = ctx.enter_context(tc.tile_pool(name="results", bufs=M_TILES * HALVES))
         psum = ctx.enter_context(tc.psum_pool(name="psum", bufs=8))
         ctx.enter_context(tc.manual_schedule())
@@ -57,15 +60,18 @@ def tile_qlstmcell_kernel(
         w_planes = {}
         c0_sb = {}
         for j in range(HALVES):
-            w_planes[j] = keep.tile([P, PASSES, 4, N_TILE], U8, name="w_planes%d" % j, align_bytes=64)
+            for c in range(PASSES):
+                w_planes[(j, c)] = keep.tile([P, 4, N_TILE], U8, name="w_planes%d_%d" % (j, c), align_bytes=64)
             c0_sb[j] = keep.tile([P, M_TILES, N_TILE], BF16, name="c0_sb%d" % j)
             for gate in GATE_ORDER:
                 w_sb[(j, gate)] = keep.tile([P, PASSES, 2 * N_TILE], U8, name="w_sb%d_%d" % (j, gate), align_bytes=64)
                 bias_sb[(j, gate)] = keep.tile([P, N_TILE], F32, name="bias_sb%d_%d" % (j, gate))
 
-        nc.vector.memset(w_planes[0][:].bitcast(I32), 0)
+        for c in range(PASSES):
+            nc.vector.memset(w_planes[(0, c)][:].bitcast(I32), 0)
         nc.vector.memset(bias_row[:].bitcast(I32), 0)
-        nc.vector.memset(w_planes[1][:].bitcast(I32), 0)
+        for c in range(PASSES):
+            nc.vector.memset(w_planes[(1, c)][:].bitcast(I32), 0)
         make_identity(nc, ident[:])
         nc.gpsimd.memset(ones[:], 1.0)
 
@@ -80,7 +86,7 @@ def tile_qlstmcell_kernel(
         def load_scales(j):
             for a in range(2):
                 for g in range(GROUPS):
-                    plane = w_planes[j][:, GROUPS * a + g, :, :]
+                    plane = w_planes[(j, GROUPS * a + g)]
                     rows = w_scales[a][g].rearrange("(q r) (t j n) -> r q t j n", r=4, t=4, j=HALVES)
                     for r in range(4):
                         nc.sync.dma_start(out=plane[r:P:32, :, :].bitcast(I32), in_=rows[r, :, :, j, :].bitcast(I32))
@@ -147,21 +153,26 @@ def tile_qlstmcell_kernel(
         cells = [(j, m) for j in range(HALVES) for m in range(M_TILES)]
         part = {}
 
-        def bank(n, gate):
+        def one_pass(acc, n, gate, c):
             j, m = cells[n]
-            acc = psum.tile([P, N_TILE], F32, name="acc", tag="bank")
-            for c in range(PASSES):
-                nc.tensor.matmul_mx(
-                    out=acc[:],
-                    lhsT=act_codes[:, m, c * P : (c + 1) * P].bitcast(FP8X4),
-                    lhsT_scale=act_planes[:, m, c * P : (c + 1) * P],
-                    rhs=w_sb[(j, gate)][:, c, :].bitcast(FP4X4),
-                    rhs_scale=w_planes[j][:, c, gate, :],
-                    start=(c == 0),
-                    stop=(c == PASSES - 1),
-                )
-            z = sums.tile([P, N_TILE], F32, name="z")
+            nc.tensor.matmul_mx(
+                out=acc[:],
+                lhsT=act_codes[:, m, c * P : (c + 1) * P].bitcast(FP8X4),
+                lhsT_scale=act_planes[:, m, c * P : (c + 1) * P],
+                rhs=w_sb[(j, gate)][:, c, :].bitcast(FP4X4),
+                rhs_scale=w_planes[(j, c)][:, gate, :],
+                start=(c == 0),
+                stop=(c == PASSES - 1),
+            )
+
+        def add_bias(pool, acc, n, gate):
+            j, m = cells[n]
+            z = pool.tile([P, N_TILE], F32, name="z")
             nc.vector.tensor_tensor(out=z[:], in0=acc[:], in1=bias_sb[(j, gate)][:], op=ALU.add)
+            part[(n, gate, "z")] = z
+
+        def half_clip(n, gate):
+            z = part[(n, gate, "z")]
             half_done = cellwise.tile([P, N_TILE], F32, name="half_done%d" % gate)
             if gate == G_GATE:
                 nc.scalar.activation(out=half_done[:], in_=z[:], func=ACT.Relu, bias=1.0, scale=1.0)
@@ -170,6 +181,13 @@ def tile_qlstmcell_kernel(
             else:
                 nc.scalar.activation(out=half_done[:], in_=z[:], func=ACT.Relu, bias=0.5, scale=1.0 / 6.0)
             part[(n, gate)] = half_done
+
+        def bank(n, gate):
+            acc = psum.tile([P, N_TILE], F32, name="acc", tag="bank")
+            for c in range(PASSES):
+                one_pass(acc, n, gate, c)
+            add_bias(sums, acc, n, gate)
+            half_clip(n, gate)
 
         def clipped_times(pool, n, name, gate, other):
             part[(n, name)] = pool.tile([P, N_TILE], F32, name=name)
@@ -198,12 +216,22 @@ def tile_qlstmcell_kernel(
             clipped_times(results, n, "h_1", O_GATE, part[(n, "tanh_c")][:])
             store(n, "h_1", out_0)
 
-        bank(0, G_GATE)
+        first = {}
+        for n in range(G_AHEAD):
+            first[n] = psum.tile([P, N_TILE], F32, name="acc", tag="bank")
+        for c in range(PASSES):
+            for n in range(G_AHEAD):
+                one_pass(first[n], n, G_GATE, c)
+        for n in range(G_AHEAD):
+            add_bias(ahead, first[n], n, G_GATE)
+        half_clip(0, G_GATE)
         for n in range(len(cells)):
             j, m = cells[n]
             bank(n, I_GATE)
             bank(n, F_GATE)
-            if n + 1 < len(cells):
+            if n + 1 < G_AHEAD:
+                half_clip(n + 1, G_GATE)
+            elif n + 1 < len(cells):
                 bank(n + 1, G_GATE)
             clipped_times(cellwise, n, "fresh", I_GATE, part[(n, G_GATE)][:])
             clipped_times(cellwise, n, "kept", F_GATE, c0_sb[j][:, m, :])

@@ -83,33 +83,44 @@ def tile_qlstmcell_kernel(
         def first_col(gate, j):
             return gate * H + j * N_TILE
 
-        def load_scales(j):
-            for a in range(2):
-                for g in range(GROUPS):
-                    plane = w_planes[(j, GROUPS * a + g)]
-                    rows = w_scales[a][g].rearrange("(q r) (t j n) -> r q t j n", r=4, t=4, j=HALVES)
-                    for r in range(4):
-                        nc.sync.dma_start(out=plane[r:P:32, :, :].bitcast(I32), in_=rows[r, :, :, j, :].bitcast(I32))
+        def load_scales(j, c):
+            a, g = divmod(c, GROUPS)
+            rows = w_scales[a][g].rearrange("(q r) (t j n) -> r q t j n", r=4, t=4, j=HALVES)
+            for r in range(4):
+                nc.sync.dma_start(out=w_planes[(j, c)][r:P:32, :, :].bitcast(I32), in_=rows[r, :, :, j, :].bitcast(I32))
 
-        def load_weights(j, gate):
+        def load_weights(j, gate, a):
             lo = first_col(gate, j)
             some_bytes = slice(2 * lo, 2 * (lo + N_TILE))
-            for a in range(2):
-                nc.sync.dma_start(
-                    out=w_sb[(j, gate)][:, GROUPS * a : GROUPS * (a + 1), :].bitcast(I32),
-                    in_=w_words[a][:, :, some_bytes].bitcast(I32).rearrange("g p n -> p g n"),
-                )
+            nc.sync.dma_start(
+                out=w_sb[(j, gate)][:, GROUPS * a : GROUPS * (a + 1), :].bitcast(I32),
+                in_=w_words[a][:, :, some_bytes].bitcast(I32).rearrange("g p n -> p g n"),
+            )
 
         def load_c0(j):
             cols = slice(j * N_TILE, (j + 1) * N_TILE)
             nc.sync.dma_start(out=c0_sb[j][:], in_=c_0.rearrange("(m p) h -> p m h", p=P)[:, :, cols])
 
-        for j in range(HALVES):
-            load_weights(j, GATE_ORDER[0])
-            load_scales(j)
-            for gate in GATE_ORDER[1:]:
-                load_weights(j, gate)
-            load_c0(j)
+        load_scales(0, 0)
+        load_weights(0, GATE_ORDER[0], 0)
+        load_scales(0, 1)
+        load_weights(0, GATE_ORDER[0], 1)
+        load_scales(0, 2)
+        load_weights(0, GATE_ORDER[1], 0)
+        load_scales(0, 3)
+        load_weights(0, GATE_ORDER[1], 1)
+        for gate in GATE_ORDER[2:]:
+            for a in range(2):
+                load_weights(0, gate, a)
+        load_c0(0)
+        for a in range(2):
+            load_weights(1, GATE_ORDER[0], a)
+        for c in range(PASSES):
+            load_scales(1, c)
+        for gate in GATE_ORDER[1:]:
+            for a in range(2):
+                load_weights(1, gate, a)
+        load_c0(1)
 
         grouped = {}
 

@@ -55,7 +55,7 @@ def tile_qlstmcell_kernel(
         ident = keep.tile([P, P], F32)
         w_sb = {}
         bias_sb = {}
-        bias_row = keep.tile([P, 4 * H], BF16)
+        bias_row = keep.tile([P, 4, N_TILE], BF16)
         ones = keep.tile([P, P], BF16)
         w_planes = {}
         c0_sb = {}
@@ -65,20 +65,24 @@ def tile_qlstmcell_kernel(
             c0_sb[j] = keep.tile([P, M_TILES, N_TILE], BF16, name="c0_sb%d" % j)
             for gate in GATE_ORDER:
                 w_sb[(j, gate)] = keep.tile([P, PASSES, 2 * N_TILE], U8, name="w_sb%d_%d" % (j, gate), align_bytes=64)
-                bias_sb[(j, gate)] = keep.tile([P, N_TILE], F32, name="bias_sb%d_%d" % (j, gate))
+                bias_sb[(j, gate)] = keep.tile([P, N_TILE], F32 if j == 0 else BF16, name="bias_sb%d_%d" % (j, gate))
 
-        for c in range(PASSES):
-            nc.vector.memset(w_planes[(0, c)][:].bitcast(I32), 0)
         nc.vector.memset(bias_row[:].bitcast(I32), 0)
         for c in range(PASSES):
-            nc.vector.memset(w_planes[(1, c)][:].bitcast(I32), 0)
+            nc.vector.memset(w_planes[(0, c)][:].bitcast(I32), 0)
         make_identity(nc, ident[:])
         nc.gpsimd.memset(ones[:], 1.0)
+        for c in range(PASSES):
+            nc.gpsimd.memset(w_planes[(1, c)][:].bitcast(U32), 0)
+        nc.scalar.dma_start(
+            out=bias_row[0:1, :, :], in_=b_hh.rearrange("(o t j n) -> j o t n", o=1, t=4, j=HALVES)[0]
+        )
+        first_of_scalar = keep.tile([P, 1], BF16)
+        nc.scalar.copy(out=first_of_scalar[:], in_=ones[:, 0:1])
 
         for m in range(M_TILES):
             for a in range(2):
                 nc.sync.dma_start(out=act_sb[:, a, m, :], in_=acts[a][m * P : (m + 1) * P, :])
-        nc.scalar.dma_start(out=bias_row[0:1, :], in_=b_hh.unsqueeze(0))
 
         def first_col(gate, j):
             return gate * H + j * N_TILE
@@ -113,6 +117,9 @@ def tile_qlstmcell_kernel(
             for a in range(2):
                 load_weights(0, gate, a)
         load_c0(0)
+        for gate in GATE_ORDER:
+            lo = first_col(gate, 1)
+            nc.sync.dma_start(out=bias_sb[(1, gate)][:], in_=b_hh[lo : lo + N_TILE].partition_broadcast(P))
         for a in range(2):
             load_weights(1, GATE_ORDER[0], a)
         for c in range(PASSES):
@@ -148,18 +155,19 @@ def tile_qlstmcell_kernel(
                 in_=grouped[m][:].rearrange("p a k -> p (a k)"),
             )
 
+        def spread_bias(gate):
+            spread = psum.tile([P, N_TILE], F32, name="spread", tag="bank")
+            nc.tensor.matmul(spread[:], lhsT=ones[:], rhs=bias_row[:, gate, :], start=True, stop=True)
+            nc.scalar.copy(out=bias_sb[(0, gate)][:], in_=spread[:])
+
         for m in range(M_TILES + 1):
             if m < M_TILES:
                 flip(m)
             if m > 0:
                 quantise(m - 1)
-
-        for j in range(HALVES):
-            for gate in GATE_ORDER:
-                lo = first_col(gate, j)
-                spread = psum.tile([P, N_TILE], F32, name="spread", tag="bank")
-                nc.tensor.matmul(spread[:], lhsT=ones[:], rhs=bias_row[:, lo : lo + N_TILE], start=True, stop=True)
-                nc.scalar.copy(out=bias_sb[(j, gate)][:], in_=spread[:])
+            if m in (1, 2):
+                for gate in GATE_ORDER[2 * (m - 1) : 2 * m]:
+                    spread_bias(gate)
 
         cells = [(j, m) for j in range(HALVES) for m in range(M_TILES)]
         part = {}

@@ -28,6 +28,9 @@ GATE_ORDER = (G_GATE, I_GATE, F_GATE, O_GATE)
 
 G_AHEAD = M_TILES
 
+ALL_COLUMNS = slice(0, N_TILE)
+COLUMN_PARTS = [slice(0, N_TILE // 2), slice(N_TILE // 2, N_TILE)]
+
 FLOPS = 2 * BATCH * (2 * K) * (4 * H)
 
 
@@ -184,52 +187,78 @@ def tile_qlstmcell_kernel(
                 stop=(c == PASSES - 1),
             )
 
-        def add_bias(pool, acc, n, gate):
-            j, m = cells[n]
-            z = pool.tile([P, N_TILE], F32, name="z")
-            nc.vector.tensor_tensor(out=z[:], in0=acc[:], in1=bias_sb[(j, gate)][:], op=ALU.add)
-            part[(n, gate, "z")] = z
+        def part_tile(pool, n, name, kind):
+            if (n, name) not in part:
+                part[(n, name)] = pool.tile([P, N_TILE], F32, name=kind)
+            return part[(n, name)]
 
-        def half_clip(n, gate):
-            z = part[(n, gate, "z")]
-            half_done = cellwise.tile([P, N_TILE], F32, name="half_done%d" % gate)
+        def add_bias(pool, acc, n, gate, cols=ALL_COLUMNS):
+            j, m = cells[n]
+            z = part_tile(pool, n, "z%d" % gate, "z")
+            nc.vector.tensor_tensor(out=z[:, cols], in0=acc[:, cols], in1=bias_sb[(j, gate)][:, cols], op=ALU.add)
+
+        def half_clip(n, gate, cols=ALL_COLUMNS):
+            z = part[(n, "z%d" % gate)]
+            half_done = part_tile(cellwise, n, gate, "half_done%d" % gate)
             if gate == G_GATE:
                 nc.scalar.activation(out=half_done[:], in_=z[:], func=ACT.Relu, bias=1.0, scale=1.0)
                 nc.scalar.activation(out=half_done[:], in_=half_done[:], func=ACT.Relu, bias=2.0, scale=-1.0)
                 nc.scalar.activation(out=half_done[:], in_=half_done[:], func=ACT.Identity, bias=1.0, scale=-1.0)
             else:
-                nc.scalar.activation(out=half_done[:], in_=z[:], func=ACT.Relu, bias=0.5, scale=1.0 / 6.0)
-            part[(n, gate)] = half_done
+                nc.scalar.activation(
+                    out=half_done[:, cols], in_=z[:, cols], func=ACT.Relu, bias=0.5, scale=1.0 / 6.0
+                )
 
-        def bank(n, gate):
+        def fill(n, gate):
             acc = psum.tile([P, N_TILE], F32, name="acc", tag="bank")
             for c in range(PASSES):
                 one_pass(acc, n, gate, c)
-            add_bias(sums, acc, n, gate)
+            return acc
+
+        def bank(n, gate):
+            add_bias(sums, fill(n, gate), n, gate)
             half_clip(n, gate)
 
-        def clipped_times(pool, n, name, gate, other):
-            part[(n, name)] = pool.tile([P, N_TILE], F32, name=name)
+        def clipped_times(pool, n, name, gate, other, cols=ALL_COLUMNS):
             nc.vector.scalar_tensor_tensor(
-                out=part[(n, name)][:], in0=part[(n, gate)][:], scalar=1.0, in1=other, op0=ALU.min, op1=ALU.mult
+                out=part_tile(pool, n, name, name)[:, cols],
+                in0=part[(n, gate)][:, cols],
+                scalar=1.0,
+                in1=other[:, cols],
+                op0=ALU.min,
+                op1=ALU.mult,
             )
 
-        def store(n, name, out):
+        def store(n, name, out, cols=ALL_COLUMNS):
             j, m = cells[n]
+            first_column = j * N_TILE
             nc.sync.dma_start(
-                out=out[m * P : (m + 1) * P, j * N_TILE : (j + 1) * N_TILE], in_=part[(n, name)][:]
+                out=out[m * P : (m + 1) * P, first_column + cols.start : first_column + cols.stop],
+                in_=part[(n, name)][:, cols],
             )
 
-        def new_cell_state(n, engine):
-            part[(n, "c_1")] = results.tile([P, N_TILE], F32, name="c_1")
+        def add_up(engine, n, cols=ALL_COLUMNS):
             engine.tensor_tensor(
-                out=part[(n, "c_1")][:], in0=part[(n, "kept")][:], in1=part[(n, "fresh")][:], op=ALU.add
+                out=part_tile(results, n, "c_1", "c_1")[:, cols],
+                in0=part[(n, "kept")][:, cols],
+                in1=part[(n, "fresh")][:, cols],
+                op=ALU.add,
             )
-            store(n, "c_1", out_1)
-            part[(n, "tanh_c")] = cellwise.tile([P, N_TILE], F32, name="tanh_c")
+
+        def clip_up(engine, n, cols=ALL_COLUMNS):
             engine.tensor_scalar(
-                out=part[(n, "tanh_c")][:], in0=part[(n, "c_1")][:], scalar1=1.0, scalar2=-1.0, op0=ALU.min, op1=ALU.max
+                out=part_tile(cellwise, n, "tanh_c", "tanh_c")[:, cols],
+                in0=part[(n, "c_1")][:, cols],
+                scalar1=1.0,
+                scalar2=-1.0,
+                op0=ALU.min,
+                op1=ALU.max,
             )
+
+        def new_cell_state(n):
+            add_up(nc.gpsimd, n)
+            store(n, "c_1", out_1)
+            clip_up(nc.gpsimd, n)
 
         def new_output(n):
             clipped_times(results, n, "h_1", O_GATE, part[(n, "tanh_c")][:])
@@ -244,6 +273,7 @@ def tile_qlstmcell_kernel(
         for n in range(G_AHEAD):
             add_bias(ahead, first[n], n, G_GATE)
         half_clip(0, G_GATE)
+        last = len(cells) - 1
         for n in range(len(cells)):
             j, m = cells[n]
             bank(n, I_GATE)
@@ -256,6 +286,18 @@ def tile_qlstmcell_kernel(
             clipped_times(cellwise, n, "kept", F_GATE, c0_sb[j][:, m, :])
             if n > 0:
                 new_output(n - 1)
-            bank(n, O_GATE)
-            new_cell_state(n, nc.gpsimd if n + 1 < len(cells) else nc.vector)
-        new_output(len(cells) - 1)
+            if n != last:
+                bank(n, O_GATE)
+                new_cell_state(n)
+        acc = fill(last, O_GATE)
+        for cols in COLUMN_PARTS:
+            add_bias(sums, acc, last, O_GATE, cols)
+            half_clip(last, O_GATE, cols)
+        for cols in COLUMN_PARTS:
+            add_up(nc.vector, last, cols)
+        for cols in COLUMN_PARTS:
+            clip_up(nc.vector, last, cols)
+        store(last, "c_1", out_1)
+        for cols in COLUMN_PARTS:
+            clipped_times(results, last, "h_1", O_GATE, part[(last, "tanh_c")][:], cols)
+            store(last, "h_1", out_0, cols)

@@ -147,15 +147,14 @@ def tile_qlstmcell_kernel(
                 dst = grouped[m][:, a, :].bitcast(F32).rearrange("p (g r u) -> p g r u", g=GROUPS, u=2)
                 src = flipped[:].rearrange("p g u r -> p g r u")
                 if a == 0:
-                    nc.vector.tensor_copy(out=dst, in_=src)
-                else:
                     nc.scalar.copy(out=dst, in_=src)
+                else:
+                    nc.vector.tensor_copy(out=dst, in_=src)
 
-        def quantise(m):
+        def quantise(m, a):
+            codes = slice(a * GROUPS * P, (a + 1) * GROUPS * P)
             nc.vector.quantize_mx(
-                out=act_codes[:, m, :].bitcast(FP8X4),
-                scales=act_planes[:, m, :],
-                in_=grouped[m][:].rearrange("p a k -> p (a k)"),
+                out=act_codes[:, m, codes].bitcast(FP8X4), scales=act_planes[:, m, codes], in_=grouped[m][:, a, :]
             )
 
         def spread_bias(gate):
@@ -163,14 +162,12 @@ def tile_qlstmcell_kernel(
             nc.tensor.matmul(spread[:], lhsT=ones[:], rhs=bias_row[:, gate, :], start=True, stop=True)
             nc.scalar.copy(out=bias_sb[(0, gate)][:], in_=spread[:])
 
-        for m in range(M_TILES + 1):
-            if m < M_TILES:
-                flip(m)
-            if m > 0:
-                quantise(m - 1)
-            if m in (1, 2):
-                for gate in GATE_ORDER[2 * (m - 1) : 2 * m]:
-                    spread_bias(gate)
+        for m in range(M_TILES):
+            flip(m)
+            for a in range(2):
+                quantise(m, a)
+        for gate in GATE_ORDER:
+            spread_bias(gate)
 
         cells = [(j, m) for j in range(HALVES) for m in range(M_TILES)]
         part = {}

@@ -90,10 +90,10 @@ def tile_qlstmcell_kernel(
         def first_col(gate, j):
             return gate * H + j * N_TILE
 
-        def load_scales(j, c):
+        def load_scales(j, c, some_r=range(4)):
             a, g = divmod(c, GROUPS)
             rows = w_scales[a][g].rearrange("(q r) (t j n) -> r q t j n", r=4, t=4, j=HALVES)
-            for r in range(4):
+            for r in some_r:
                 nc.sync.dma_start(out=w_planes[(j, c)][r:P:32, :, :].bitcast(I32), in_=rows[r, :, :, j, :].bitcast(I32))
 
         def load_weights(j, gate, a):
@@ -120,16 +120,13 @@ def tile_qlstmcell_kernel(
             for a in range(2):
                 load_weights(0, gate, a)
         load_c0(0)
+        for gate, c in zip(GATE_ORDER, range(PASSES)):
+            for a in range(2):
+                load_weights(1, gate, a)
+                load_scales(1, c, range(2 * a, 2 * a + 2))
         for gate in GATE_ORDER:
             lo = first_col(gate, 1)
             nc.sync.dma_start(out=bias_sb[(1, gate)][:], in_=b_hh[lo : lo + N_TILE].partition_broadcast(P))
-        for a in range(2):
-            load_weights(1, GATE_ORDER[0], a)
-        for c in range(PASSES):
-            load_scales(1, c)
-        for gate in GATE_ORDER[1:]:
-            for a in range(2):
-                load_weights(1, gate, a)
         load_c0(1)
 
         grouped = {}

@@ -104,9 +104,11 @@ def tile_qlstmcell_kernel(
                 in_=w_words[a][:, :, some_bytes].bitcast(I32).rearrange("g p n -> p g n"),
             )
 
-        def load_c0(j):
+        def load_c0(j, some_m):
             cols = slice(j * N_TILE, (j + 1) * N_TILE)
-            nc.sync.dma_start(out=c0_sb[j][:], in_=c_0.rearrange("(m p) h -> p m h", p=P)[:, :, cols])
+            nc.sync.dma_start(
+                out=c0_sb[j][:, some_m, :], in_=c_0.rearrange("(m p) h -> p m h", p=P)[:, some_m, cols]
+            )
 
         load_scales(0, 0)
         load_weights(0, GATE_ORDER[0], 0)
@@ -116,18 +118,28 @@ def tile_qlstmcell_kernel(
         load_weights(0, GATE_ORDER[1], 0)
         load_scales(0, 3)
         load_weights(0, GATE_ORDER[1], 1)
-        for gate in GATE_ORDER[2:]:
-            for a in range(2):
-                load_weights(0, gate, a)
-        load_c0(0)
-        for gate, c in zip(GATE_ORDER, range(PASSES)):
-            for a in range(2):
-                load_weights(1, gate, a)
-                load_scales(1, c, range(2 * a, 2 * a + 2))
+        for a in range(2):
+            load_weights(0, GATE_ORDER[2], a)
+        large_loads = (
+            lambda: load_weights(0, GATE_ORDER[3], 0),
+            lambda: load_weights(0, GATE_ORDER[3], 1),
+            lambda: load_c0(0, slice(0, M_TILES // 2)),
+            lambda: load_weights(1, GATE_ORDER[0], 0),
+            lambda: load_weights(1, GATE_ORDER[0], 1),
+            lambda: load_c0(0, slice(M_TILES // 2, M_TILES)),
+            lambda: load_weights(1, GATE_ORDER[1], 0),
+            lambda: load_weights(1, GATE_ORDER[1], 1),
+        )
+        for i, load in enumerate(large_loads):
+            load()
+            load_scales(1, i // 2, range(2 * (i % 2), 2 * (i % 2) + 2))
         for gate in GATE_ORDER:
             lo = first_col(gate, 1)
             nc.sync.dma_start(out=bias_sb[(1, gate)][:], in_=b_hh[lo : lo + N_TILE].partition_broadcast(P))
-        load_c0(1)
+        for gate in GATE_ORDER[2:]:
+            for a in range(2):
+                load_weights(1, gate, a)
+        load_c0(1, slice(0, M_TILES))
 
         grouped = {}
 

@@ -58,8 +58,8 @@ def tile_qlstmcell_kernel(
         ident = keep.tile([P, P], F32)
         w_sb = {}
         bias_sb = {}
-        bias_row = keep.tile([P, 4, N_TILE], BF16)
-        ones = keep.tile([P, P], BF16)
+        bias_rows = keep.tile([P, N_TILE], BF16)
+        pick = keep.tile([P, P], BF16)
         w_planes = {}
         c0_sb = {}
         for j in range(HALVES):
@@ -68,20 +68,18 @@ def tile_qlstmcell_kernel(
             c0_sb[j] = keep.tile([P, M_TILES, N_TILE], BF16, name="c0_sb%d" % j)
             for gate in GATE_ORDER:
                 w_sb[(j, gate)] = keep.tile([P, PASSES, 2 * N_TILE], U8, name="w_sb%d_%d" % (j, gate), align_bytes=64)
-                bias_sb[(j, gate)] = keep.tile([P, N_TILE], F32 if j == 0 else BF16, name="bias_sb%d_%d" % (j, gate))
+                bias_sb[(j, gate)] = keep.tile([P, N_TILE], F32, name="bias_sb%d_%d" % (j, gate))
 
-        nc.vector.memset(bias_row[:].bitcast(I32), 0)
+        nc.vector.memset(bias_rows[:].bitcast(I32), 0)
         for c in range(PASSES):
             nc.vector.memset(w_planes[(0, c)][:].bitcast(I32), 0)
         make_identity(nc, ident[:])
-        nc.gpsimd.memset(ones[:], 1.0)
+        make_identity(nc, pick[:])
         for c in range(PASSES):
             nc.gpsimd.memset(w_planes[(1, c)][:].bitcast(U32), 0)
-        nc.scalar.dma_start(
-            out=bias_row[0:1, :, :], in_=b_hh.rearrange("(o t j n) -> j o t n", o=1, t=4, j=HALVES)[0]
-        )
+        nc.scalar.dma_start(out=bias_rows[0 : 4 * HALVES, :], in_=b_hh.rearrange("(r n) -> r n", n=N_TILE))
         first_of_scalar = keep.tile([P, 1], BF16)
-        nc.scalar.copy(out=first_of_scalar[:], in_=ones[:, 0:1])
+        nc.scalar.copy(out=first_of_scalar[:], in_=pick[:, 0:1])
 
         for m in range(M_TILES):
             for a in range(2):
@@ -133,9 +131,6 @@ def tile_qlstmcell_kernel(
         for i, load in enumerate(large_loads):
             load()
             load_scales(1, i // 2, range(2 * (i % 2), 2 * (i % 2) + 2))
-        for gate in GATE_ORDER:
-            lo = first_col(gate, 1)
-            nc.sync.dma_start(out=bias_sb[(1, gate)][:], in_=b_hh[lo : lo + N_TILE].partition_broadcast(P))
         for gate in GATE_ORDER[2:]:
             for a in range(2):
                 load_weights(1, gate, a)
@@ -143,22 +138,20 @@ def tile_qlstmcell_kernel(
 
         grouped = {}
 
-        def flip(m):
-            grouped[m] = stage.tile([P, 2, K], BF16, name="grouped", align_bytes=64)
-            for a in range(2):
-                words = act_sb[:, a, m, :].bitcast(F32)
-                flipped = psum.tile([P, GROUPS, 2, P], F32, name="flipped", tag="bank")
-                for g in range(GROUPS):
-                    for u in range(2):
-                        nc.tensor.transpose(
-                            flipped[:, g, u, :], words[:, 2 * P * g + u : 2 * P * (g + 1) : 2], ident[:]
-                        )
-                dst = grouped[m][:, a, :].bitcast(F32).rearrange("p (g r u) -> p g r u", g=GROUPS, u=2)
-                src = flipped[:].rearrange("p g u r -> p g r u")
-                if a == 0:
-                    nc.scalar.copy(out=dst, in_=src)
-                else:
-                    nc.vector.tensor_copy(out=dst, in_=src)
+        def flip(m, a):
+            words = act_sb[:, a, m, :].bitcast(F32)
+            flipped = psum.tile([P, GROUPS, 2, P], F32, name="flipped", tag="bank")
+            for g in range(GROUPS):
+                for u in range(2):
+                    nc.tensor.transpose(
+                        flipped[:, g, u, :], words[:, 2 * P * g + u : 2 * P * (g + 1) : 2], ident[:]
+                    )
+            dst = grouped[m][:, a, :].bitcast(F32).rearrange("p (g r u) -> p g r u", g=GROUPS, u=2)
+            src = flipped[:].rearrange("p g u r -> p g r u")
+            if a == 0:
+                nc.scalar.copy(out=dst, in_=src)
+            else:
+                nc.vector.tensor_copy(out=dst, in_=src)
 
         def quantise(m, a):
             codes = slice(a * GROUPS * P, (a + 1) * GROUPS * P)
@@ -166,17 +159,23 @@ def tile_qlstmcell_kernel(
                 out=act_codes[:, m, codes].bitcast(FP8X4), scales=act_planes[:, m, codes], in_=grouped[m][:, a, :]
             )
 
-        def spread_bias(gate):
+        def spread_bias(j, gate):
+            r = HALVES * gate + j
             spread = psum.tile([P, N_TILE], F32, name="spread", tag="bank")
-            nc.tensor.matmul(spread[:], lhsT=ones[:], rhs=bias_row[:, gate, :], start=True, stop=True)
-            nc.scalar.copy(out=bias_sb[(0, gate)][:], in_=spread[:])
+            nc.tensor.matmul(
+                spread[:], lhsT=pick[:, r : r + 1].to_broadcast([P, P]), rhs=bias_rows[:], start=True, stop=True
+            )
+            nc.scalar.copy(out=bias_sb[(j, gate)][:], in_=spread[:])
 
+        biases = [(j, gate) for j in range(HALVES) for gate in GATE_ORDER]
         for m in range(M_TILES):
-            flip(m)
+            grouped[m] = stage.tile([P, 2, K], BF16, name="grouped", align_bytes=64)
+            for a in range(2):
+                flip(m, a)
+                for i in range(min(m, 1) + m // (M_TILES - 1)):
+                    spread_bias(*biases.pop(0))
             for a in range(2):
                 quantise(m, a)
-        for gate in GATE_ORDER:
-            spread_bias(gate)
 
         cells = [(j, m) for j in range(HALVES) for m in range(M_TILES)]
         part = {}

@@ -111,29 +111,27 @@ def tile_qlstmcell_kernel(
         load_scales(0, 0)
         load_weights(0, GATE_ORDER[0], 0)
         load_scales(0, 1)
-        load_weights(0, GATE_ORDER[0], 1)
         load_scales(0, 2)
-        load_weights(0, GATE_ORDER[1], 0)
+        load_weights(0, GATE_ORDER[0], 1)
         load_scales(0, 3)
-        load_weights(0, GATE_ORDER[1], 1)
-        for a in range(2):
-            load_weights(0, GATE_ORDER[2], a)
+        for gate in GATE_ORDER[1:]:
+            for a in range(2):
+                load_weights(0, gate, a)
         large_loads = (
-            lambda: load_weights(0, GATE_ORDER[3], 0),
-            lambda: load_weights(0, GATE_ORDER[3], 1),
             lambda: load_c0(0, slice(0, M_TILES // 2)),
             lambda: load_weights(1, GATE_ORDER[0], 0),
             lambda: load_weights(1, GATE_ORDER[0], 1),
             lambda: load_c0(0, slice(M_TILES // 2, M_TILES)),
             lambda: load_weights(1, GATE_ORDER[1], 0),
             lambda: load_weights(1, GATE_ORDER[1], 1),
+            lambda: load_weights(1, GATE_ORDER[2], 0),
+            lambda: load_weights(1, GATE_ORDER[2], 1),
         )
         for i, load in enumerate(large_loads):
             load()
             load_scales(1, i // 2, range(2 * (i % 2), 2 * (i % 2) + 2))
-        for gate in GATE_ORDER[2:]:
-            for a in range(2):
-                load_weights(1, gate, a)
+        for a in range(2):
+            load_weights(1, GATE_ORDER[3], a)
         load_c0(1, slice(0, M_TILES))
 
         grouped = {}
@@ -197,12 +195,12 @@ def tile_qlstmcell_kernel(
                 part[(n, name)] = pool.tile([P, N_TILE], F32, name=kind)
             return part[(n, name)]
 
-        def add_bias(pool, acc, n, gate, cols=ALL_COLUMNS):
+        def add_bias(pool, acc, n, gate):
             j, m = cells[n]
             z = part_tile(pool, n, "z%d" % gate, "z")
-            nc.vector.tensor_tensor(out=z[:, cols], in0=acc[:, cols], in1=bias_sb[(j, gate)][:, cols], op=ALU.add)
+            nc.vector.tensor_tensor(out=z[:], in0=acc[:], in1=bias_sb[(j, gate)][:], op=ALU.add)
 
-        def half_clip(n, gate, cols=ALL_COLUMNS):
+        def half_clip(n, gate):
             z = part[(n, "z%d" % gate)]
             half_done = part_tile(cellwise, n, gate, "half_done%d" % gate)
             if gate == G_GATE:
@@ -210,9 +208,7 @@ def tile_qlstmcell_kernel(
                 nc.scalar.activation(out=half_done[:], in_=half_done[:], func=ACT.Relu, bias=2.0, scale=-1.0)
                 nc.scalar.activation(out=half_done[:], in_=half_done[:], func=ACT.Identity, bias=1.0, scale=-1.0)
             else:
-                nc.scalar.activation(
-                    out=half_done[:, cols], in_=z[:, cols], func=ACT.Relu, bias=0.5, scale=1.0 / 6.0
-                )
+                nc.scalar.activation(out=half_done[:], in_=z[:], func=ACT.Relu, bias=0.5, scale=1.0 / 6.0)
 
         def fill(n, gate):
             acc = psum.tile([P, N_TILE], F32, name="acc", tag="bank")
@@ -242,12 +238,9 @@ def tile_qlstmcell_kernel(
                 in_=part[(n, name)][:, cols],
             )
 
-        def add_up(engine, n, cols=ALL_COLUMNS):
+        def add_up(engine, n):
             engine.tensor_tensor(
-                out=part_tile(results, n, "c_1", "c_1")[:, cols],
-                in0=part[(n, "kept")][:, cols],
-                in1=part[(n, "fresh")][:, cols],
-                op=ALU.add,
+                out=part_tile(results, n, "c_1", "c_1")[:], in0=part[(n, "kept")][:], in1=part[(n, "fresh")][:], op=ALU.add
             )
 
         def clip_up(engine, n, cols=ALL_COLUMNS):
@@ -289,20 +282,17 @@ def tile_qlstmcell_kernel(
                 bank(n + 1, G_GATE)
             clipped_times(cellwise, n, "fresh", I_GATE, part[(n, G_GATE)][:])
             clipped_times(cellwise, n, "kept", F_GATE, c0_sb[j][:, m, :])
-            if n > 0:
-                new_output(n - 1)
             if n != last:
+                if n > 0:
+                    new_output(n - 1)
                 bank(n, O_GATE)
                 new_cell_state(n)
-        acc = fill(last, O_GATE)
-        for cols in COLUMN_PARTS:
-            add_bias(sums, acc, last, O_GATE, cols)
-            half_clip(last, O_GATE, cols)
-        for cols in COLUMN_PARTS:
-            add_up(nc.vector, last, cols)
+        bank(last, O_GATE)
+        add_up(nc.vector, last)
+        store(last, "c_1", out_1)
+        new_output(last - 1)
         for cols in COLUMN_PARTS:
             clip_up(nc.vector, last, cols)
-        store(last, "c_1", out_1)
         for cols in COLUMN_PARTS:
             clipped_times(results, last, "h_1", O_GATE, part[(last, "tanh_c")][:], cols)
             store(last, "h_1", out_0, cols)

from contextlib import ExitStack

import concourse.mybir as mybir
from concourse.masks import make_identity

F32 = mybir.dt.float32
BF16 = mybir.dt.bfloat16
I32 = mybir.dt.int32
U32 = mybir.dt.uint32
U8 = mybir.dt.uint8
FP8X4 = mybir.dt.float8_e4m3fn_x4
FP4X4 = mybir.dt.float4_e2m1fn_x4
ALU = mybir.AluOpType
ACT = mybir.ActivationFunctionType

P = 128
BATCH = 512
K = 1024
H = 1024
M_TILES = BATCH // P
K_PASS = 4 * P
GROUPS = K // K_PASS
PASSES = 2 * GROUPS
N_TILE = 512
HALVES = H // N_TILE
F_GATE, I_GATE, O_GATE, G_GATE = 0, 1, 2, 3
GATE_ORDER = (G_GATE, I_GATE, F_GATE, O_GATE)

G_AHEAD = M_TILES

ALL_COLUMNS = slice(0, N_TILE)
COLUMN_PARTS = [slice(0, N_TILE // 2), slice(N_TILE // 2, N_TILE)]

FLOPS = 2 * BATCH * (2 * K) * (4 * H)


def tile_qlstmcell_kernel(
    tc, input_, h_0, c_0, W_ih_words, W_ih_scales, W_hh_words, W_hh_scales, b_hh, out_0, out_1
):
    nc = tc.nc
    acts = (input_, h_0)
    w_words = (W_ih_words, W_hh_words)
    w_scales = (W_ih_scales, W_hh_scales)

    with ExitStack() as ctx:
        keep = ctx.enter_context(tc.tile_pool(name="keep", bufs=1))
        stage = ctx.enter_context(tc.tile_pool(name="stage", bufs=M_TILES))
        sums = ctx.enter_context(tc.tile_pool(name="sums", bufs=6))
        cellwise = ctx.enter_context(tc.tile_pool(name="cellwise", bufs=2))
        ahead = ctx.enter_context(tc.tile_pool(name="ahead", bufs=G_AHEAD))
        results = ctx.enter_context(tc.tile_pool(name="results", bufs=M_TILES * HALVES))
        psum = ctx.enter_context(tc.psum_pool(name="psum", bufs=8))
        ctx.enter_context(tc.manual_schedule())

        act_sb = keep.tile([P, 2, M_TILES, K], BF16)
        act_codes = keep.tile([P, M_TILES, PASSES * P], U32, align_bytes=64)
        act_planes = keep.tile([P, M_TILES, PASSES * P], U8, align_bytes=64)
        ident = keep.tile([P, P], F32)
        w_sb = {}
        bias_sb = {}
        bias_rows = keep.tile([P, N_TILE], BF16)
        pick = keep.tile([P, P], BF16)
        w_planes = {}
        c0_sb = {}
        for j in range(HALVES):
            for c in range(PASSES):
                w_planes[(j, c)] = keep.tile([P, 4, N_TILE], U8, name="w_planes%d_%d" % (j, c), align_bytes=64)
            c0_sb[j] = keep.tile([P, M_TILES, N_TILE], BF16, name="c0_sb%d" % j)
            for gate in GATE_ORDER:
                w_sb[(j, gate)] = keep.tile([P, PASSES, 2 * N_TILE], U8, name="w_sb%d_%d" % (j, gate), align_bytes=64)
                bias_sb[(j, gate)] = keep.tile([P, N_TILE], F32, name="bias_sb%d_%d" % (j, gate))

        nc.vector.memset(bias_rows[:].bitcast(I32), 0)
        for c in range(PASSES):
            nc.vector.memset(w_planes[(0, c)][:].bitcast(I32), 0)
        make_identity(nc, ident[:])
        make_identity(nc, pick[:])
        for c in range(PASSES):
            nc.gpsimd.memset(w_planes[(1, c)][:].bitcast(U32), 0)
        nc.scalar.dma_start(out=bias_rows[0 : 4 * HALVES, :], in_=b_hh.rearrange("(r n) -> r n", n=N_TILE))
        first_of_scalar = keep.tile([P, 1], BF16)
        nc.scalar.copy(out=first_of_scalar[:], in_=pick[:, 0:1])

        for m in range(M_TILES):
            for a in range(2):
                nc.sync.dma_start(out=act_sb[:, a, m, :], in_=acts[a][m * P : (m + 1) * P, :])

        def first_col(gate, j):
            return gate * H + j * N_TILE

        def load_scales(j, c, some_r=range(4)):
            a, g = divmod(c, GROUPS)
            rows = w_scales[a][g].rearrange("(q r) (t j n) -> r q t j n", r=4, t=4, j=HALVES)
            for r in some_r:
                nc.sync.dma_start(out=w_planes[(j, c)][r:P:32, :, :].bitcast(I32), in_=rows[r, :, :, j, :].bitcast(I32))

        def load_weights(j, gate, a):
            lo = first_col(gate, j)
            some_bytes = slice(2 * lo, 2 * (lo + N_TILE))
            nc.sync.dma_start(
                out=w_sb[(j, gate)][:, GROUPS * a : GROUPS * (a + 1), :].bitcast(I32),
                in_=w_words[a][:, :, some_bytes].bitcast(I32).rearrange("g p n -> p g n"),
            )

        def load_c0(j, some_m):
            cols = slice(j * N_TILE, (j + 1) * N_TILE)
            nc.sync.dma_start(
                out=c0_sb[j][:, some_m, :], in_=c_0.rearrange("(m p) h -> p m h", p=P)[:, some_m, cols]
            )

        load_scales(0, 0)
        load_weights(0, GATE_ORDER[0], 0)
        load_scales(0, 1)
        load_scales(0, 2)
        load_weights(0, GATE_ORDER[0], 1)
        load_scales(0, 3)
        for gate in GATE_ORDER[1:]:
            for a in range(2):
                load_weights(0, gate, a)
        large_loads = (
            lambda: load_c0(0, slice(0, M_TILES // 2)),
            lambda: load_weights(1, GATE_ORDER[0], 0),
            lambda: load_weights(1, GATE_ORDER[0], 1),
            lambda: load_c0(0, slice(M_TILES // 2, M_TILES)),
            lambda: load_weights(1, GATE_ORDER[1], 0),
            lambda: load_weights(1, GATE_ORDER[1], 1),
            lambda: load_weights(1, GATE_ORDER[2], 0),
            lambda: load_weights(1, GATE_ORDER[2], 1),
        )
        for i, load in enumerate(large_loads):
            load()
            load_scales(1, i // 2, range(2 * (i % 2), 2 * (i % 2) + 2))
        for a in range(2):
            load_weights(1, GATE_ORDER[3], a)
        load_c0(1, slice(0, M_TILES))

        grouped = {}

        def flip(m, a):
            words = act_sb[:, a, m, :].bitcast(F32)
            flipped = psum.tile([P, GROUPS, 2, P], F32, name="flipped", tag="bank")
            for g in range(GROUPS):
                for u in range(2):
                    nc.tensor.transpose(
                        flipped[:, g, u, :], words[:, 2 * P * g + u : 2 * P * (g + 1) : 2], ident[:]
                    )
            dst = grouped[m][:, a, :].bitcast(F32).rearrange("p (g r u) -> p g r u", g=GROUPS, u=2)
            src = flipped[:].rearrange("p g u r -> p g r u")
            if a == 0:
                nc.scalar.copy(out=dst, in_=src)
            else:
                nc.vector.tensor_copy(out=dst, in_=src)

        def quantise(m, a):
            codes = slice(a * GROUPS * P, (a + 1) * GROUPS * P)
            nc.vector.quantize_mx(
                out=act_codes[:, m, codes].bitcast(FP8X4), scales=act_planes[:, m, codes], in_=grouped[m][:, a, :]
            )

        def spread_bias(j, gate):
            r = HALVES * gate + j
            spread = psum.tile([P, N_TILE], F32, name="spread", tag="bank")
            nc.tensor.matmul(
                spread[:], lhsT=pick[:, r : r + 1].to_broadcast([P, P]), rhs=bias_rows[:], start=True, stop=True
            )
            nc.scalar.copy(out=bias_sb[(j, gate)][:], in_=spread[:])

        biases = [(j, gate) for j in range(HALVES) for gate in GATE_ORDER]
        for m in range(M_TILES):
            grouped[m] = stage.tile([P, 2, K], BF16, name="grouped", align_bytes=64)
            for a in range(2):
                flip(m, a)
                for i in range(min(m, 1) + m // (M_TILES - 1)):
                    spread_bias(*biases.pop(0))
            for a in range(2):
                quantise(m, a)

        cells = [(j, m) for j in range(HALVES) for m in range(M_TILES)]
        part = {}

        def one_pass(acc, n, gate, c):
            j, m = cells[n]
            nc.tensor.matmul_mx(
                out=acc[:],
                lhsT=act_codes[:, m, c * P : (c + 1) * P].bitcast(FP8X4),
                lhsT_scale=act_planes[:, m, c * P : (c + 1) * P],
                rhs=w_sb[(j, gate)][:, c, :].bitcast(FP4X4),
                rhs_scale=w_planes[(j, c)][:, gate, :],
                start=(c == 0),
                stop=(c == PASSES - 1),
            )

        def part_tile(pool, n, name, kind):
            if (n, name) not in part:
                part[(n, name)] = pool.tile([P, N_TILE], F32, name=kind)
            return part[(n, name)]

        def add_bias(pool, acc, n, gate):
            j, m = cells[n]
            z = part_tile(pool, n, "z%d" % gate, "z")
            nc.vector.tensor_tensor(out=z[:], in0=acc[:], in1=bias_sb[(j, gate)][:], op=ALU.add)

        def half_clip(n, gate):
            z = part[(n, "z%d" % gate)]
            half_done = part_tile(cellwise, n, gate, "half_done%d" % gate)
            if gate == G_GATE:
                nc.scalar.activation(out=half_done[:], in_=z[:], func=ACT.Relu, bias=1.0, scale=1.0)
                nc.scalar.activation(out=half_done[:], in_=half_done[:], func=ACT.Relu, bias=2.0, scale=-1.0)
                nc.scalar.activation(out=half_done[:], in_=half_done[:], func=ACT.Identity, bias=1.0, scale=-1.0)
            else:
                nc.scalar.activation(out=half_done[:], in_=z[:], func=ACT.Relu, bias=0.5, scale=1.0 / 6.0)

        def fill(n, gate):
            acc = psum.tile([P, N_TILE], F32, name="acc", tag="bank")
            for c in range(PASSES):
                one_pass(acc, n, gate, c)
            return acc

        def bank(n, gate):
            add_bias(sums, fill(n, gate), n, gate)
            half_clip(n, gate)

        def clipped_times(pool, n, name, gate, other, cols=ALL_COLUMNS):
            nc.vector.scalar_tensor_tensor(
                out=part_tile(pool, n, name, name)[:, cols],
                in0=part[(n, gate)][:, cols],
                scalar=1.0,
                in1=other[:, cols],
                op0=ALU.min,
                op1=ALU.mult,
            )

        def store(n, name, out, cols=ALL_COLUMNS):
            j, m = cells[n]
            first_column = j * N_TILE
            nc.sync.dma_start(
                out=out[m * P : (m + 1) * P, first_column + cols.start : first_column + cols.stop],
                in_=part[(n, name)][:, cols],
            )

        def add_up(engine, n):
            engine.tensor_tensor(
                out=part_tile(results, n, "c_1", "c_1")[:], in0=part[(n, "kept")][:], in1=part[(n, "fresh")][:], op=ALU.add
            )

        def clip_up(engine, n, cols=ALL_COLUMNS):
            engine.tensor_scalar(
                out=part_tile(cellwise, n, "tanh_c", "tanh_c")[:, cols],
                in0=part[(n, "c_1")][:, cols],
                scalar1=1.0,
                scalar2=-1.0,
                op0=ALU.min,
                op1=ALU.max,
            )

        def new_cell_state(n):
            add_up(nc.gpsimd, n)
            store(n, "c_1", out_1)
            clip_up(nc.gpsimd, n)

        def new_output(n):
            clipped_times(results, n, "h_1", O_GATE, part[(n, "tanh_c")][:])
            store(n, "h_1", out_0)

        first = {}
        for n in range(G_AHEAD):
            first[n] = psum.tile([P, N_TILE], F32, name="acc", tag="bank")
        for c in range(PASSES):
            for n in range(G_AHEAD):
                one_pass(first[n], n, G_GATE, c)
        for n in range(G_AHEAD):
            add_bias(ahead, first[n], n, G_GATE)
        half_clip(0, G_GATE)
        last = len(cells) - 1
        for n in range(len(cells)):
            j, m = cells[n]
            bank(n, I_GATE)
            bank(n, F_GATE)
            if n + 1 < G_AHEAD:
                half_clip(n + 1, G_GATE)
            elif n + 1 < len(cells):
                bank(n + 1, G_GATE)
            clipped_times(cellwise, n, "fresh", I_GATE, part[(n, G_GATE)][:])
            clipped_times(cellwise, n, "kept", F_GATE, c0_sb[j][:, m, :])
            if n != last:
                if n > 0:
                    new_output(n - 1)
                bank(n, O_GATE)
                new_cell_state(n)
        bank(last, O_GATE)
        add_up(nc.vector, last)
        store(last, "c_1", out_1)
        new_output(last - 1)
        for cols in COLUMN_PARTS:
            clip_up(nc.vector, last, cols)
        for cols in COLUMN_PARTS:
            clipped_times(results, last, "h_1", O_GATE, part[(last, "tanh_c")][:], cols)
            store(last, "h_1", out_0, cols)
